import numpy as np
import ml_dtypes


def mxq(x, axis, fmt="e4m3"):
    dtype, down = {"e4m3": (ml_dtypes.float8_e4m3fn, 7), "e5m2": (ml_dtypes.float8_e5m2, 14)}[fmt]
    v = np.moveaxis(np.asarray(x, np.float32).astype(ml_dtypes.bfloat16).astype(np.float64), axis, -1)
    blocks = v.reshape(v.shape[:-1] + (-1, 32))
    amax = np.abs(blocks).max(-1, keepdims=True)
    byte = np.maximum(np.where(amax > 0, np.frexp(amax)[1] - 1 + 127, 0) - down, 1)
    scale = np.exp2(byte - 127.0)
    codes = (blocks / scale).astype(np.float32).astype(dtype).astype(np.float64)
    return np.moveaxis((codes * scale).reshape(v.shape), -1, axis)


WIDE = False


def mx_kscale(k):
    if not WIDE:
        return np.ones(k)
    levels = np.array([10, -10, 5, -5, 0])
    a = np.random.permutation(np.resize(levels, k // 512 * 4)).reshape(k // 512, 4)
    idx = np.arange(k)
    return np.exp2(a[idx // 512, idx % 128 // 32])


BF16 = ml_dtypes.bfloat16


def bf(x):
    return np.asarray(x, np.float32).astype(BF16)


def f64(x):
    return np.asarray(x).astype(np.float64)


E2M1 = np.array([0.0, 0.5, 1.0, 1.5, 2.0, 3.0, 4.0, 6.0, -0.0, -0.5, -1.0, -1.5, -2.0, -3.0, -4.0, -6.0])


def pack_weight(w, fmt):
    k, n = w.shape
    w = f64(bf(w)).reshape(k // 32, 32, n)
    amax = np.abs(w).max(1)
    if fmt == "e4m3":
        byte = np.frexp(amax)[1] - 1 + 127 - 7
    else:
        mant, ex = np.frexp(amax / 6.0)
        byte = np.where(mant > 0.5, ex, ex - 1) + 127
    byte = np.clip(np.where(amax > 0, byte, 1), 1, 254)
    scaled = (w * np.exp2(127.0 - byte)[:, None, :]).reshape(k, n).astype(np.float32)
    by_word = np.ascontiguousarray(scaled.reshape(k // 512, 128, 4, n).transpose(0, 1, 3, 2))
    if fmt == "e4m3":
        words = by_word.astype(ml_dtypes.float8_e4m3fn).view(np.uint8)
    else:
        c = by_word.astype(ml_dtypes.float4_e2m1fn).view(np.uint8) & 0xF
        words = c[..., 0::2] | (c[..., 1::2] << 4)
    return np.ascontiguousarray(words), np.ascontiguousarray(byte.astype(np.uint8).reshape(k // 512, 16, n))


def unpack_weight(words, scales, fmt):
    g, p, n, _ = words.shape
    if fmt == "e4m3":
        vals = np.ascontiguousarray(words).view(ml_dtypes.float8_e4m3fn).astype(np.float64)
    else:
        nib = np.empty((g, p, n, 4), np.uint8)
        nib[..., 0::2] = words & 0xF
        nib[..., 1::2] = words >> 4
        vals = E2M1[nib]
    vals = vals * np.repeat(np.exp2(scales.astype(np.float64) - 127.0), 8, axis=1)[..., None]
    return vals.transpose(0, 1, 3, 2).reshape(g * 512, n)

def pack4(w):
    words, scales = pack_weight(w, "e2m1")
    return words.reshape(words.shape[0], 128, -1), scales


def unpack4(words, scales):
    return unpack_weight(words.reshape(words.shape[0], 128, -1, 2), scales, "e2m1")


B, T, HS, C, NH, HD, WS, MAXD = 1, 8, 28, 512, 32, 16, 7, 3
N = T * HS * HS
E = NH * HD
BT = B * NH * T
EPS = 1e-12


def l2norm(v, axis):
    return v / np.maximum(np.sqrt(np.sum(v * v, axis=axis, keepdims=True)), EPS)


def setup_inputs():
    s = mx_kscale(C)
    x = bf(np.random.standard_normal((B, N, C)) * s)
    q_w_words, q_w_scales = pack4((np.random.standard_normal((E, C)) / np.sqrt(C) / s).T)
    k_w_words, k_w_scales = pack4((np.random.standard_normal((E, C)) / np.sqrt(C) / s).T)
    return {"x": x,
            "q_w_words": q_w_words, "q_w_scales": q_w_scales,
            "k_w_words": k_w_words, "k_w_scales": k_w_scales}


def reference(x, q_w_words, q_w_scales, k_w_words, k_w_scales):
    xq = mxq(f64(x), 2, "e4m3")
    q = xq @ unpack4(q_w_words, q_w_scales)
    k = xq @ unpack4(k_w_words, k_w_scales)
    q = q.reshape(B, N, NH, HD).transpose(0, 2, 1, 3)
    k = k.reshape(B, N, NH, HD).transpose(0, 2, 1, 3)
    q = q.reshape(B * NH, T, HS, HS, HD).transpose(0, 1, 4, 2, 3)
    k = k.reshape(B * NH, T, HS, HS, HD).transpose(0, 1, 4, 2, 3)
    k_post = np.concatenate([k[:, 1:], k[:, -1:]], axis=1)
    qp = l2norm(q.reshape(BT, HD, HS, HS), 1)
    kp = l2norm(k_post.reshape(BT, HD, HS, HS), 1)
    return qp, kp

@@ -1,0 +1,228 @@
+from contextlib import ExitStack
+
+import concourse.mybir as mybir
+from concourse.masks import make_identity
+
+F32 = mybir.dt.float32
+BF16 = mybir.dt.bfloat16
+I32 = mybir.dt.int32
+U32 = mybir.dt.uint32
+U8 = mybir.dt.uint8
+FP8X4 = mybir.dt.float8_e4m3fn_x4
+FP4X4 = mybir.dt.float4_e2m1fn_x4
+ACT = mybir.ActivationFunctionType
+ALU = mybir.AluOpType
+AXIS = mybir.AxisListType
+
+P = 128
+FRAMES = 8
+POSITIONS = 784
+CHANNELS = 512
+HEADS = 32
+HEAD_DIM = 16
+QUARTERS = 4
+RUN = 4
+TOKENS = 128
+BODY = 768
+TAIL = POSITIONS - BODY
+MAX_INVERSE_NORM = 1.0e12
+
+FLOPS = 2 * FRAMES * POSITIONS * CHANNELS * 2 * HEADS * HEAD_DIM
+
+CHUNKS = BODY // (2 * P)
+TURN_LEAD = 6
+QUANTISE_LEAD = 3
+NORM_LAG = 4
+SCALE_LAG = 5
+QUANT_BUFS = 6
+WORK_BUFS = 8
+
+def load_weight(nc, consts, words, scales, label):
+    raw_words = consts.tile([P, 2 * CHANNELS], U8, name="raw_words_" + label)
+    nc.sync.dma_start(out=raw_words[:].bitcast(I32), in_=words[0].bitcast(I32))
+    raw_scales = consts.tile([P, CHANNELS], U8, name="raw_scales_" + label)
+    nc.vector.memset(raw_scales[:].bitcast(I32), 0)
+    for quadrant in range(4):
+        nc.sync.dma_start(
+            out=raw_scales[32 * quadrant : 32 * quadrant + 4, :].bitcast(I32),
+            in_=scales[0, 4 * quadrant : 4 * quadrant + 4, :].bitcast(I32),
+        )
+    w_words = consts.tile([P, 2 * CHANNELS], U8, name="w_words_" + label, align_bytes=64)
+    nc.vector.tensor_copy(
+        out=w_words[:].bitcast(I32).rearrange("p (j h c) -> p j h c", j=QUARTERS, c=2),
+        in_=raw_words[:].bitcast(I32).rearrange("p (h j c) -> p j h c", j=QUARTERS, c=2),
+    )
+    w_scales = consts.tile([P, CHANNELS], U8, name="w_scales_" + label, align_bytes=64)
+    nc.vector.tensor_copy(
+        out=w_scales[:].bitcast(I32).rearrange("p (j h) -> p j h", j=QUARTERS),
+        in_=raw_scales[:].bitcast(I32).rearrange("p (h j) -> p j h", j=QUARTERS),
+    )
+    return w_words, w_scales
+
+
+def tile_costvolumeattention17_pa_kernel(
+    tc, x, q_w_words, q_w_scales, k_w_words, k_w_scales, out_0, out_1
+):
+    nc = tc.nc
+    tokens = x[0]
+    with ExitStack() as ctx:
+        consts = ctx.enter_context(tc.tile_pool(name="consts", bufs=1))
+        x_pool = ctx.enter_context(tc.tile_pool(name="x_pool", bufs=1))
+        quant = ctx.enter_context(tc.tile_pool(name="quant", bufs=QUANT_BUFS))
+        work = ctx.enter_context(tc.tile_pool(name="work", bufs=WORK_BUFS))
+        frames_out = ctx.enter_context(tc.tile_pool(name="frames_out", bufs=4))
+        psum = ctx.enter_context(tc.psum_pool(name="psum", bufs=8))
+        ctx.enter_context(tc.manual_schedule())
+
+        x_raw = {}
+        x_raw["tail"] = x_pool.tile([P, 1, CHANNELS], BF16, name="x_tail")
+        nc.sync.dma_start(
+            out=x_raw["tail"][:, 0, :],
+            in_=tokens.rearrange("(t n) c -> t n c", t=FRAMES)[:, BODY:POSITIONS, :],
+        )
+        weights = {
+            "q": load_weight(nc, consts, q_w_words, q_w_scales, "q"),
+            "k": load_weight(nc, consts, k_w_words, k_w_scales, "k"),
+        }
+        for f in range(FRAMES):
+            for s in range(CHUNKS):
+                first = f * POSITIONS + s * 2 * P
+                x_raw[(f, s)] = x_pool.tile([P, 2, CHANNELS], BF16, name="x_raw_%d_%d" % (f, s))
+                nc.sync.dma_start(
+                    out=x_raw[(f, s)][:],
+                    in_=tokens[first : first + 2 * P, :].rearrange("(p b) c -> p b c", b=2),
+                )
+
+        ident = consts.tile([P, P], F32, name="ident")
+        make_identity(nc, ident[:])
+        group_sel = consts.tile([P, HEADS], F32, name="group_sel")
+        nc.vector.tensor_reduce(
+            out=group_sel[:], in_=ident[:].rearrange("p (g r) -> p g r", r=RUN), axis=AXIS.X, op=ALU.add
+        )
+        group_ones = consts.tile([P, HEADS, RUN], F32, name="group_ones")
+        nc.vector.tensor_copy(out=group_ones[:], in_=group_sel[:].unsqueeze(2).to_broadcast([P, HEADS, RUN]))
+        tails = {
+            "q": consts.tile([P, QUARTERS, FRAMES, TAIL], F32, name="tails_q"),
+            "k": consts.tile([P, QUARTERS, FRAMES, TAIL], F32, name="tails_k"),
+        }
+        rows = {
+            "q": out_0.rearrange("(h t) (j r) a b -> t j h r (a b)", t=FRAMES, r=RUN),
+            "k": out_1.rearrange("(h t) (j r) a b -> t j h r (a b)", t=FRAMES, r=RUN),
+        }
+
+        units = [("tail", 0, "q", None, 0), ("tail", 0, "k", None, 0)]
+        for f in range(FRAMES):
+            for name in ("k", "q") if f > 0 else ("q",):
+                for s in range(CHUNKS):
+                    for half in range(2):
+                        units.append(((f, s), half * TOKENS, name, f, s * 2 * P + half * TOKENS))
+        first_use = {}
+        for index, unit in enumerate(units):
+            if unit[0] not in first_use:
+                first_use[unit[0]] = index
+        chunk_used_first_at = dict((index, chunk) for chunk, index in first_use.items())
+
+        grouped_of = {}
+        quantised = {}
+        acc_of = {}
+        pairs_of = {}
+        inverse_of = {}
+        result = {}
+
+        def turn(chunk):
+            raw = x_raw[chunk]
+            blocks = raw.shape[1]
+            turned = psum.tile([P, blocks, 2, P], F32, name="turned", tag="bank")
+            for b in range(blocks):
+                for u in range(2):
+                    nc.tensor.transpose(
+                        turned[:, b, u, :], raw[:, b, :].bitcast(F32)[:, u : CHANNELS // 2 : 2], ident[:]
+                    )
+            grouped = quant.tile([P, blocks * P * 4], BF16, name="grouped", tag="grouped", align_bytes=64)
+            nc.scalar.copy(
+                out=grouped[:].bitcast(F32).rearrange("p (c b u) -> p c b u", b=blocks, u=2),
+                in_=turned[:].rearrange("p b u c -> p c b u"),
+            )
+            grouped_of[chunk] = grouped
+
+        def quantise(chunk):
+            grouped = grouped_of[chunk]
+            width = grouped.shape[1] // 4
+            codes = quant.tile([P, width], U32, name="codes", tag="codes", align_bytes=64)
+            scales = quant.tile([P, width], U8, name="scales", tag="scales", align_bytes=64)
+            nc.vector.quantize_mx(out=codes[:].bitcast(FP8X4), scales=scales[:], in_=grouped[:])
+            quantised[chunk] = (codes, scales)
+
+        def project(index):
+            chunk, column, name, frame, first = units[index]
+            codes, scales = quantised[chunk]
+            w_words, w_scales = weights[name]
+            acc = psum.tile([P, QUARTERS, TOKENS], F32, name="acc", tag="bank")
+            for j in range(QUARTERS):
+                nc.tensor.matmul_mx(
+                    out=acc[:, j, :],
+                    lhsT=w_words[:, 2 * P * j : 2 * P * (j + 1)].bitcast(FP4X4),
+                    lhsT_scale=w_scales[:, P * j : P * (j + 1)],
+                    rhs=codes[:, column : column + TOKENS].bitcast(FP8X4),
+                    rhs_scale=scales[:, column : column + TOKENS],
+                    start=True,
+                    stop=True,
+                )
+            squares = work.tile([P, QUARTERS, TOKENS], F32, name="squares")
+            nc.scalar.activation(out=squares[:], in_=acc[:], func=ACT.Square)
+            pairs = work.tile([P, 2, TOKENS], F32, name="pairs")
+            nc.gpsimd.tensor_tensor(out=pairs[:], in0=squares[:, 0:2, :], in1=squares[:, 2:4, :], op=ALU.add)
+            acc_of[index] = acc
+            pairs_of[index] = pairs
+
+        def invert_norm(index):
+            pairs = pairs_of[index]
+            partial = work.tile([P, TOKENS], F32, name="partial")
+            nc.vector.tensor_tensor(out=partial[:], in0=pairs[:, 0, :], in1=pairs[:, 1, :], op=ALU.add)
+            total = psum.tile([P, TOKENS], F32, name="total", tag="bank")
+            nc.tensor.matmul(
+                out=total[:], lhsT=group_ones[:].rearrange("p g r -> p (g r)"), rhs=partial[:], start=True, stop=True
+            )
+            inverse = work.tile([P, TOKENS], F32, name="inverse")
+            nc.scalar.activation(out=inverse[:], in_=total[:], func=ACT.Abs_reciprocal_sqrt)
+            inverse_of[index] = inverse
+
+        def scale(index):
+            chunk, column, name, frame, first = units[index]
+            if frame is None:
+                dest = tails[name][:].rearrange("p j t i -> p j (t i)")
+            else:
+                if first == 0:
+                    result[name] = frames_out.tile([P, QUARTERS, POSITIONS], F32, name="result")
+                    nc.gpsimd.tensor_copy(out=result[name][:, :, BODY:POSITIONS], in_=tails[name][:, :, frame, :])
+                dest = result[name][:, :, first : first + TOKENS]
+            nc.vector.scalar_tensor_tensor(
+                out=dest,
+                in0=inverse_of[index][:].unsqueeze(1).to_broadcast([P, QUARTERS, TOKENS]),
+                scalar=MAX_INVERSE_NORM,
+                in1=acc_of[index][:],
+                op0=ALU.min,
+                op1=ALU.mult,
+            )
+            if frame is not None and first + TOKENS == BODY:
+                if name == "q":
+                    targets = [frame]
+                elif frame == FRAMES - 1:
+                    targets = [frame - 1, frame]
+                else:
+                    targets = [frame - 1]
+                for t in targets:
+                    for j in range(QUARTERS):
+                        nc.sync.dma_start(out=rows[name][t, j], in_=result[name][:, j, :])
+
+        for step in range(-TURN_LEAD, len(units) + SCALE_LAG):
+            if step + TURN_LEAD in chunk_used_first_at:
+                turn(chunk_used_first_at[step + TURN_LEAD])
+            if step + QUANTISE_LEAD in chunk_used_first_at:
+                quantise(chunk_used_first_at[step + QUANTISE_LEAD])
+            if 0 <= step < len(units):
+                project(step)
+            if 0 <= step - NORM_LAG < len(units):
+                invert_norm(step - NORM_LAG)
+            if 0 <= step - SCALE_LAG < len(units):
+                scale(step - SCALE_LAG)

@@ -32,7 +32,7 @@ FLOPS = 2 * FRAMES * POSITIONS * CHANNELS * 2 * HEADS * HEAD_DIM
 CHUNKS = BODY // (2 * P)
 TURN_LEAD = 6
 QUANTISE_LEAD = 3
-NORM_LAG = 4
+NORM_LAG = 3
 SCALE_LAG = 5
 QUANT_BUFS = 6
 WORK_BUFS = 8

@@ -30,12 +30,13 @@ MAX_INVERSE_NORM = 1.0e12
 FLOPS = 2 * FRAMES * POSITIONS * CHANNELS * 2 * HEADS * HEAD_DIM
 
 CHUNKS = BODY // (2 * P)
-TURN_LEAD = 6
-QUANTISE_LEAD = 3
-NORM_LAG = 3
-SCALE_LAG = 5
-QUANT_BUFS = 6
-WORK_BUFS = 8
+TURN_LEAD = 3
+QUANTISE_LEAD = 2
+ADD_LAG = 2
+NORM_LAG = 4
+SCALE_LAG = 4
+GROUPED_BUFS = 3
+WORK_BUFS = 5
 
 def load_weight(nc, consts, words, scales, label):
     raw_words = consts.tile([P, 2 * CHANNELS], U8, name="raw_words_" + label)
@@ -68,7 +69,8 @@ def tile_costvolumeattention17_pa_kernel(
     with ExitStack() as ctx:
         consts = ctx.enter_context(tc.tile_pool(name="consts", bufs=1))
         x_pool = ctx.enter_context(tc.tile_pool(name="x_pool", bufs=1))
-        quant = ctx.enter_context(tc.tile_pool(name="quant", bufs=QUANT_BUFS))
+        quant = ctx.enter_context(tc.tile_pool(name="quant", bufs=1))
+        grouped_pool = ctx.enter_context(tc.tile_pool(name="grouped_pool", bufs=GROUPED_BUFS))
         work = ctx.enter_context(tc.tile_pool(name="work", bufs=WORK_BUFS))
         frames_out = ctx.enter_context(tc.tile_pool(name="frames_out", bufs=4))
         psum = ctx.enter_context(tc.psum_pool(name="psum", bufs=8))
@@ -110,12 +112,11 @@ def tile_costvolumeattention17_pa_kernel(
             "k": out_1.rearrange("(h t) (j r) a b -> t j h r (a b)", t=FRAMES, r=RUN),
         }
 
-        units = [("tail", 0, "q", None, 0), ("tail", 0, "k", None, 0)]
+        units = [("tail", "q", None, 0), ("tail", "k", None, 0)]
         for f in range(FRAMES):
             for name in ("k", "q") if f > 0 else ("q",):
                 for s in range(CHUNKS):
-                    for half in range(2):
-                        units.append(((f, s), half * TOKENS, name, f, s * 2 * P + half * TOKENS))
+                    units.append(((f, s), name, f, s * 2 * P))
         first_use = {}
         for index, unit in enumerate(units):
             if unit[0] not in first_use:
@@ -124,8 +125,8 @@ def tile_costvolumeattention17_pa_kernel(
 
         grouped_of = {}
         quantised = {}
-        acc_of = {}
         pairs_of = {}
+        partial_of = {}
         inverse_of = {}
         result = {}
 
@@ -138,7 +139,7 @@ def tile_costvolumeattention17_pa_kernel(
                     nc.tensor.transpose(
                         turned[:, b, u, :], raw[:, b, :].bitcast(F32)[:, u : CHANNELS // 2 : 2], ident[:]
                     )
-            grouped = quant.tile([P, blocks * P * 4], BF16, name="grouped", tag="grouped", align_bytes=64)
+            grouped = grouped_pool.tile([P, blocks * P * 4], BF16, name="grouped", align_bytes=64)
             nc.scalar.copy(
                 out=grouped[:].bitcast(F32).rearrange("p (c b u) -> p c b u", b=blocks, u=2),
                 in_=turned[:].rearrange("p b u c -> p c b u"),
@@ -148,63 +149,78 @@ def tile_costvolumeattention17_pa_kernel(
         def quantise(chunk):
             grouped = grouped_of[chunk]
             width = grouped.shape[1] // 4
-            codes = quant.tile([P, width], U32, name="codes", tag="codes", align_bytes=64)
-            scales = quant.tile([P, width], U8, name="scales", tag="scales", align_bytes=64)
+            label = "tail" if chunk == "tail" else "%d_%d" % chunk
+            codes = quant.tile([P, width], U32, name="codes_" + label, align_bytes=64)
+            scales = quant.tile([P, width], U8, name="scales_" + label, align_bytes=64)
             nc.vector.quantize_mx(out=codes[:].bitcast(FP8X4), scales=scales[:], in_=grouped[:])
             quantised[chunk] = (codes, scales)
 
-        def project(index):
-            chunk, column, name, frame, first = units[index]
-            codes, scales = quantised[chunk]
-            w_words, w_scales = weights[name]
-            acc = psum.tile([P, QUARTERS, TOKENS], F32, name="acc", tag="bank")
-            for j in range(QUARTERS):
+        def project(index, bank):
+            codes, scales = quantised[units[index][0]]
+            w_words, w_scales = weights[units[index][1]]
+            acc = psum.tile([P, 2, codes.shape[1]], F32, name="acc", tag="bank")
+            for i in range(2):
+                j = 2 * bank + i
                 nc.tensor.matmul_mx(
-                    out=acc[:, j, :],
+                    out=acc[:, i, :],
                     lhsT=w_words[:, 2 * P * j : 2 * P * (j + 1)].bitcast(FP4X4),
                     lhsT_scale=w_scales[:, P * j : P * (j + 1)],
-                    rhs=codes[:, column : column + TOKENS].bitcast(FP8X4),
-                    rhs_scale=scales[:, column : column + TOKENS],
+                    rhs=codes[:].bitcast(FP8X4),
+                    rhs_scale=scales[:],
                     start=True,
                     stop=True,
                 )
-            squares = work.tile([P, QUARTERS, TOKENS], F32, name="squares")
-            nc.scalar.activation(out=squares[:], in_=acc[:], func=ACT.Square)
-            pairs = work.tile([P, 2, TOKENS], F32, name="pairs")
+            return acc
+
+        def square(index):
+            width = quantised[units[index][0]][0].shape[1]
+            squares = work.tile([P, QUARTERS, width], F32, name="squares", tag="squares")
+            for bank in range(2):
+                acc = project(index, bank)
+                nc.scalar.activation(out=squares[:, 2 * bank : 2 * bank + 2, :], in_=acc[:], func=ACT.Square)
+            pairs = work.tile([P, 2, width], F32, name="pairs", tag="pairs")
             nc.gpsimd.tensor_tensor(out=pairs[:], in0=squares[:, 0:2, :], in1=squares[:, 2:4, :], op=ALU.add)
-            acc_of[index] = acc
             pairs_of[index] = pairs
 
-        def invert_norm(index):
+        def add_pairs(index):
             pairs = pairs_of[index]
-            partial = work.tile([P, TOKENS], F32, name="partial")
+            partial = work.tile([P, pairs.shape[2]], F32, name="partial", tag="partial")
             nc.vector.tensor_tensor(out=partial[:], in0=pairs[:, 0, :], in1=pairs[:, 1, :], op=ALU.add)
-            total = psum.tile([P, TOKENS], F32, name="total", tag="bank")
+            partial_of[index] = partial
+
+        def invert_norm(index):
+            partial = partial_of[index]
+            width = partial.shape[1]
+            total = psum.tile([P, width], F32, name="total", tag="bank")
             nc.tensor.matmul(
                 out=total[:], lhsT=group_ones[:].rearrange("p g r -> p (g r)"), rhs=partial[:], start=True, stop=True
             )
-            inverse = work.tile([P, TOKENS], F32, name="inverse")
+            inverse = work.tile([P, width], F32, name="inverse", tag="inverse")
             nc.scalar.activation(out=inverse[:], in_=total[:], func=ACT.Abs_reciprocal_sqrt)
             inverse_of[index] = inverse
 
         def scale(index):
-            chunk, column, name, frame, first = units[index]
+            chunk, name, frame, first = units[index]
+            inverse = inverse_of[index]
+            width = inverse.shape[1]
             if frame is None:
                 dest = tails[name][:].rearrange("p j t i -> p j (t i)")
             else:
                 if first == 0:
                     result[name] = frames_out.tile([P, QUARTERS, POSITIONS], F32, name="result")
                     nc.gpsimd.tensor_copy(out=result[name][:, :, BODY:POSITIONS], in_=tails[name][:, :, frame, :])
-                dest = result[name][:, :, first : first + TOKENS]
-            nc.vector.scalar_tensor_tensor(
-                out=dest,
-                in0=inverse_of[index][:].unsqueeze(1).to_broadcast([P, QUARTERS, TOKENS]),
-                scalar=MAX_INVERSE_NORM,
-                in1=acc_of[index][:],
-                op0=ALU.min,
-                op1=ALU.mult,
-            )
-            if frame is not None and first + TOKENS == BODY:
+                dest = result[name][:, :, first : first + width]
+            for bank in range(2):
+                acc = project(index, bank)
+                nc.vector.scalar_tensor_tensor(
+                    out=dest[:, 2 * bank : 2 * bank + 2, :],
+                    in0=inverse[:].unsqueeze(1).to_broadcast([P, 2, width]),
+                    scalar=MAX_INVERSE_NORM,
+                    in1=acc[:],
+                    op0=ALU.min,
+                    op1=ALU.mult,
+                )
+            if frame is not None and first + width == BODY:
                 if name == "q":
                     targets = [frame]
                 elif frame == FRAMES - 1:
@@ -221,7 +237,9 @@ def tile_costvolumeattention17_pa_kernel(
             if step + QUANTISE_LEAD in chunk_used_first_at:
                 quantise(chunk_used_first_at[step + QUANTISE_LEAD])
             if 0 <= step < len(units):
-                project(step)
+                square(step)
+            if 0 <= step - ADD_LAG < len(units):
+                add_pairs(step - ADD_LAG)
             if 0 <= step - NORM_LAG < len(units):
                 invert_norm(step - NORM_LAG)
             if 0 <= step - SCALE_LAG < len(units):

@@ -32,11 +32,12 @@ FLOPS = 2 * FRAMES * POSITIONS * CHANNELS * 2 * HEADS * HEAD_DIM
 CHUNKS = BODY // (2 * P)
 TURN_LEAD = 3
 QUANTISE_LEAD = 2
-ADD_LAG = 2
-NORM_LAG = 4
-SCALE_LAG = 4
+ADD_LAG = 1
+NORM_LAG = 3
+SCALE_LAG = 3
 GROUPED_BUFS = 3
-WORK_BUFS = 5
+SQUARES_BUFS = 2
+WORK_BUFS = 4
 
 def load_weight(nc, consts, words, scales, label):
     raw_words = consts.tile([P, 2 * CHANNELS], U8, name="raw_words_" + label)
@@ -71,10 +72,16 @@ def tile_costvolumeattention17_pa_kernel(
         x_pool = ctx.enter_context(tc.tile_pool(name="x_pool", bufs=1))
         quant = ctx.enter_context(tc.tile_pool(name="quant", bufs=1))
         grouped_pool = ctx.enter_context(tc.tile_pool(name="grouped_pool", bufs=GROUPED_BUFS))
+        squares_pool = ctx.enter_context(tc.tile_pool(name="squares_pool", bufs=SQUARES_BUFS))
         work = ctx.enter_context(tc.tile_pool(name="work", bufs=WORK_BUFS))
         frames_out = ctx.enter_context(tc.tile_pool(name="frames_out", bufs=4))
         psum = ctx.enter_context(tc.psum_pool(name="psum", bufs=8))
         ctx.enter_context(tc.manual_schedule())
+
+        groups = [("tail", ("q", "k"), None, 0)]
+        for f in reversed(range(FRAMES)):
+            for s in range(CHUNKS):
+                groups.append(((f, s), ("q", "k") if f > 0 else ("q",), f, s * 2 * P))
 
         x_raw = {}
         x_raw["tail"] = x_pool.tile([P, 1, CHANNELS], BF16, name="x_tail")
@@ -86,14 +93,14 @@ def tile_costvolumeattention17_pa_kernel(
             "q": load_weight(nc, consts, q_w_words, q_w_scales, "q"),
             "k": load_weight(nc, consts, k_w_words, k_w_scales, "k"),
         }
-        for f in range(FRAMES):
-            for s in range(CHUNKS):
-                first = f * POSITIONS + s * 2 * P
-                x_raw[(f, s)] = x_pool.tile([P, 2, CHANNELS], BF16, name="x_raw_%d_%d" % (f, s))
-                nc.sync.dma_start(
-                    out=x_raw[(f, s)][:],
-                    in_=tokens[first : first + 2 * P, :].rearrange("(p b) c -> p b c", b=2),
-                )
+        for chunk, names, f, first in groups[1:]:
+            x_raw[chunk] = x_pool.tile([P, 2, CHANNELS], BF16, name="x_raw_%d_%d" % chunk)
+            nc.sync.dma_start(
+                out=x_raw[chunk][:],
+                in_=tokens[f * POSITIONS + first : f * POSITIONS + first + 2 * P, :].rearrange(
+                    "(p b) c -> p b c", b=2
+                ),
+            )
 
         ident = consts.tile([P, P], F32, name="ident")
         make_identity(nc, ident[:])
@@ -112,26 +119,22 @@ def tile_costvolumeattention17_pa_kernel(
             "k": out_1.rearrange("(h t) (j r) a b -> t j h r (a b)", t=FRAMES, r=RUN),
         }
 
-        units = [("tail", "q", None, 0), ("tail", "k", None, 0)]
-        for f in range(FRAMES):
-            for name in ("k", "q") if f > 0 else ("q",):
-                for s in range(CHUNKS):
-                    units.append(((f, s), name, f, s * 2 * P))
-        first_use = {}
-        for index, unit in enumerate(units):
-            if unit[0] not in first_use:
-                first_use[unit[0]] = index
-        chunk_used_first_at = dict((index, chunk) for chunk, index in first_use.items())
-
         grouped_of = {}
         quantised = {}
+        squares_of = {}
         pairs_of = {}
         partial_of = {}
         inverse_of = {}
         result = {}
 
-        def turn(chunk):
-            raw = x_raw[chunk]
+        def valid(g):
+            return 0 <= g < len(groups)
+
+        def banks(g):
+            return 2 * len(groups[g][1]) if valid(g) else 0
+
+        def turn(g):
+            raw = x_raw[groups[g][0]]
             blocks = raw.shape[1]
             turned = psum.tile([P, blocks, 2, P], F32, name="turned", tag="bank")
             for b in range(blocks):
@@ -144,23 +147,22 @@ def tile_costvolumeattention17_pa_kernel(
                 out=grouped[:].bitcast(F32).rearrange("p (c b u) -> p c b u", b=blocks, u=2),
                 in_=turned[:].rearrange("p b u c -> p c b u"),
             )
-            grouped_of[chunk] = grouped
+            grouped_of[g] = grouped
 
-        def quantise(chunk):
-            grouped = grouped_of[chunk]
+        def quantise(g):
+            grouped = grouped_of[g]
             width = grouped.shape[1] // 4
-            label = "tail" if chunk == "tail" else "%d_%d" % chunk
-            codes = quant.tile([P, width], U32, name="codes_" + label, align_bytes=64)
-            scales = quant.tile([P, width], U8, name="scales_" + label, align_bytes=64)
+            codes = quant.tile([P, width], U32, name="codes_%d" % g, align_bytes=64)
+            scales = quant.tile([P, width], U8, name="scales_%d" % g, align_bytes=64)
             nc.vector.quantize_mx(out=codes[:].bitcast(FP8X4), scales=scales[:], in_=grouped[:])
-            quantised[chunk] = (codes, scales)
+            quantised[g] = (codes, scales)
 
-        def project(index, bank):
-            codes, scales = quantised[units[index][0]]
-            w_words, w_scales = weights[units[index][1]]
+        def project(g, bank):
+            codes, scales = quantised[g]
+            w_words, w_scales = weights[groups[g][1][bank // 2]]
             acc = psum.tile([P, 2, codes.shape[1]], F32, name="acc", tag="bank")
             for i in range(2):
-                j = 2 * bank + i
+                j = 2 * (bank % 2) + i
                 nc.tensor.matmul_mx(
                     out=acc[:, i, :],
                     lhsT=w_words[:, 2 * P * j : 2 * P * (j + 1)].bitcast(FP4X4),
@@ -172,54 +174,60 @@ def tile_costvolumeattention17_pa_kernel(
                 )
             return acc
 
-        def square(index):
-            width = quantised[units[index][0]][0].shape[1]
-            squares = work.tile([P, QUARTERS, width], F32, name="squares", tag="squares")
-            for bank in range(2):
-                acc = project(index, bank)
-                nc.scalar.activation(out=squares[:, 2 * bank : 2 * bank + 2, :], in_=acc[:], func=ACT.Square)
-            pairs = work.tile([P, 2, width], F32, name="pairs", tag="pairs")
-            nc.gpsimd.tensor_tensor(out=pairs[:], in0=squares[:, 0:2, :], in1=squares[:, 2:4, :], op=ALU.add)
-            pairs_of[index] = pairs
+        def square_bank(g, bank):
+            if bank == 0:
+                width = quantised[g][0].shape[1]
+                squares_of[g] = squares_pool.tile([P, banks(g), 2, width], F32, name="squares")
+            acc = project(g, bank)
+            nc.scalar.activation(out=squares_of[g][:, bank, :, :], in_=acc[:], func=ACT.Square)
 
-        def add_pairs(index):
-            pairs = pairs_of[index]
-            partial = work.tile([P, pairs.shape[2]], F32, name="partial", tag="partial")
-            nc.vector.tensor_tensor(out=partial[:], in0=pairs[:, 0, :], in1=pairs[:, 1, :], op=ALU.add)
-            partial_of[index] = partial
+        def add_quarters(g):
+            by_weight = squares_of[g][:].rearrange("p (w b) i n -> p w b (i n)", b=2)
+            pairs = work.tile([P, by_weight.shape[1], by_weight.shape[3]], F32, name="pairs", tag="pairs")
+            nc.gpsimd.tensor_tensor(out=pairs[:], in0=by_weight[:, :, 0, :], in1=by_weight[:, :, 1, :], op=ALU.add)
+            pairs_of[g] = pairs
 
-        def invert_norm(index):
-            partial = partial_of[index]
-            width = partial.shape[1]
-            total = psum.tile([P, width], F32, name="total", tag="bank")
+        def add_pairs(g):
+            halves = pairs_of[g][:].rearrange("p w (i n) -> p w i n", i=2)
+            partial = work.tile([P, halves.shape[1], halves.shape[3]], F32, name="partial", tag="partial")
+            nc.vector.tensor_tensor(out=partial[:], in0=halves[:, :, 0, :], in1=halves[:, :, 1, :], op=ALU.add)
+            partial_of[g] = partial
+
+        def invert_norm(g):
+            partial = partial_of[g]
+            total = psum.tile(list(partial.shape), F32, name="total", tag="bank")
             nc.tensor.matmul(
-                out=total[:], lhsT=group_ones[:].rearrange("p g r -> p (g r)"), rhs=partial[:], start=True, stop=True
+                out=total[:].rearrange("p w n -> p (w n)"),
+                lhsT=group_ones[:].rearrange("p g r -> p (g r)"),
+                rhs=partial[:].rearrange("p w n -> p (w n)"),
+                start=True,
+                stop=True,
             )
-            inverse = work.tile([P, width], F32, name="inverse", tag="inverse")
+            inverse = work.tile(list(partial.shape), F32, name="inverse", tag="inverse")
             nc.scalar.activation(out=inverse[:], in_=total[:], func=ACT.Abs_reciprocal_sqrt)
-            inverse_of[index] = inverse
+            inverse_of[g] = inverse
 
-        def scale(index):
-            chunk, name, frame, first = units[index]
-            inverse = inverse_of[index]
-            width = inverse.shape[1]
+        def scale_bank(g, bank):
+            chunk, names, frame, first = groups[g]
+            name = names[bank // 2]
+            inverse = inverse_of[g]
+            width = inverse.shape[2]
             if frame is None:
                 dest = tails[name][:].rearrange("p j t i -> p j (t i)")
             else:
-                if first == 0:
+                if first == 0 and bank % 2 == 0:
                     result[name] = frames_out.tile([P, QUARTERS, POSITIONS], F32, name="result")
                     nc.gpsimd.tensor_copy(out=result[name][:, :, BODY:POSITIONS], in_=tails[name][:, :, frame, :])
                 dest = result[name][:, :, first : first + width]
-            for bank in range(2):
-                acc = project(index, bank)
-                nc.vector.scalar_tensor_tensor(
-                    out=dest[:, 2 * bank : 2 * bank + 2, :],
-                    in0=inverse[:].unsqueeze(1).to_broadcast([P, 2, width]),
-                    scalar=MAX_INVERSE_NORM,
-                    in1=acc[:],
-                    op0=ALU.min,
-                    op1=ALU.mult,
-                )
+            acc = project(g, bank)
+            nc.vector.scalar_tensor_tensor(
+                out=dest[:, 2 * (bank % 2) : 2 * (bank % 2) + 2, :],
+                in0=inverse[:, bank // 2, :].unsqueeze(1).to_broadcast([P, 2, width]),
+                scalar=MAX_INVERSE_NORM,
+                in1=acc[:],
+                op0=ALU.min,
+                op1=ALU.mult,
+            )
             if frame is not None and first + width == BODY:
                 if name == "q":
                     targets = [frame]
@@ -228,19 +236,22 @@ def tile_costvolumeattention17_pa_kernel(
                 else:
                     targets = [frame - 1]
                 for t in targets:
-                    for j in range(QUARTERS):
+                    for j in range(2 * (bank % 2), 2 * (bank % 2) + 2):
                         nc.sync.dma_start(out=rows[name][t, j], in_=result[name][:, j, :])
 
-        for step in range(-TURN_LEAD, len(units) + SCALE_LAG):
-            if step + TURN_LEAD in chunk_used_first_at:
-                turn(chunk_used_first_at[step + TURN_LEAD])
-            if step + QUANTISE_LEAD in chunk_used_first_at:
-                quantise(chunk_used_first_at[step + QUANTISE_LEAD])
-            if 0 <= step < len(units):
-                square(step)
-            if 0 <= step - ADD_LAG < len(units):
-                add_pairs(step - ADD_LAG)
-            if 0 <= step - NORM_LAG < len(units):
+        for step in range(-TURN_LEAD, len(groups) + SCALE_LAG):
+            if valid(step + TURN_LEAD):
+                turn(step + TURN_LEAD)
+            if valid(step + QUANTISE_LEAD):
+                quantise(step + QUANTISE_LEAD)
+            if valid(step - NORM_LAG):
                 invert_norm(step - NORM_LAG)
-            if 0 <= step - SCALE_LAG < len(units):
-                scale(step - SCALE_LAG)
+            for bank in range(max(banks(step), banks(step - SCALE_LAG))):
+                if bank < banks(step):
+                    square_bank(step, bank)
+                if bank < banks(step - SCALE_LAG):
+                    scale_bank(step - SCALE_LAG, bank)
+            if valid(step):
+                add_quarters(step)
+            if valid(step - ADD_LAG):
+                add_pairs(step - ADD_LAG)

@@ -31,7 +31,7 @@ FLOPS = 2 * FRAMES * POSITIONS * CHANNELS * 2 * HEADS * HEAD_DIM
 
 CHUNKS = BODY // (2 * P)
 TURN_LEAD = 3
-QUANTISE_LEAD = 2
+QUANTISE_LEAD = 3
 ADD_LAG = 1
 NORM_LAG = 3
 SCALE_LAG = 3
@@ -74,6 +74,7 @@ def tile_costvolumeattention17_pa_kernel(
         grouped_pool = ctx.enter_context(tc.tile_pool(name="grouped_pool", bufs=GROUPED_BUFS))
         squares_pool = ctx.enter_context(tc.tile_pool(name="squares_pool", bufs=SQUARES_BUFS))
         work = ctx.enter_context(tc.tile_pool(name="work", bufs=WORK_BUFS))
+        pairs_pool = ctx.enter_context(tc.tile_pool(name="pairs_pool", bufs=1))
         frames_out = ctx.enter_context(tc.tile_pool(name="frames_out", bufs=4))
         psum = ctx.enter_context(tc.psum_pool(name="psum", bufs=8))
         ctx.enter_context(tc.manual_schedule())
@@ -183,7 +184,7 @@ def tile_costvolumeattention17_pa_kernel(
 
         def add_quarters(g):
             by_weight = squares_of[g][:].rearrange("p (w b) i n -> p w b (i n)", b=2)
-            pairs = work.tile([P, by_weight.shape[1], by_weight.shape[3]], F32, name="pairs", tag="pairs")
+            pairs = pairs_pool.tile([P, by_weight.shape[1], by_weight.shape[3]], F32, name="pairs", tag="pairs")
             nc.gpsimd.tensor_tensor(out=pairs[:], in0=by_weight[:, :, 0, :], in1=by_weight[:, :, 1, :], op=ALU.add)
             pairs_of[g] = pairs
 
@@ -242,8 +243,6 @@ def tile_costvolumeattention17_pa_kernel(
         for step in range(-TURN_LEAD, len(groups) + SCALE_LAG):
             if valid(step + TURN_LEAD):
                 turn(step + TURN_LEAD)
-            if valid(step + QUANTISE_LEAD):
-                quantise(step + QUANTISE_LEAD)
             if valid(step - NORM_LAG):
                 invert_norm(step - NORM_LAG)
             for bank in range(max(banks(step), banks(step - SCALE_LAG))):
@@ -251,7 +250,9 @@ def tile_costvolumeattention17_pa_kernel(
                     square_bank(step, bank)
                 if bank < banks(step - SCALE_LAG):
                     scale_bank(step - SCALE_LAG, bank)
-            if valid(step):
-                add_quarters(step)
             if valid(step - ADD_LAG):
                 add_pairs(step - ADD_LAG)
+            if valid(step + QUANTISE_LEAD):
+                quantise(step + QUANTISE_LEAD)
+            if valid(step):
+                add_quarters(step)

@@ -25,6 +25,8 @@ RUN = 4
 TOKENS = 128
 BODY = 768
 TAIL = POSITIONS - BODY
+LATE_FRAMES = 2
+EARLY_PIECE = 512
 MAX_INVERSE_NORM = 1.0e12
 
 FLOPS = 2 * FRAMES * POSITIONS * CHANNELS * 2 * HEADS * HEAD_DIM
@@ -229,7 +231,14 @@ def tile_costvolumeattention17_pa_kernel(
                 op0=ALU.min,
                 op1=ALU.mult,
             )
-            if frame is not None and first + width == BODY:
+            early = frame is not None and frame < LATE_FRAMES
+            if early and first + width == EARLY_PIECE:
+                piece = (0, EARLY_PIECE)
+            elif frame is not None and first + width == BODY:
+                piece = (EARLY_PIECE if early else 0, POSITIONS)
+            else:
+                piece = None
+            if piece is not None:
                 if name == "q":
                     targets = [frame]
                 elif frame == FRAMES - 1:
@@ -238,7 +247,10 @@ def tile_costvolumeattention17_pa_kernel(
                     targets = [frame - 1]
                 for t in targets:
                     for j in range(2 * (bank % 2), 2 * (bank % 2) + 2):
-                        nc.sync.dma_start(out=rows[name][t, j], in_=result[name][:, j, :])
+                        nc.sync.dma_start(
+                            out=rows[name][t, j][:, :, piece[0] : piece[1]],
+                            in_=result[name][:, j, piece[0] : piece[1]],
+                        )
 
         for step in range(-TURN_LEAD, len(groups) + SCALE_LAG):
             if valid(step + TURN_LEAD):

@@ -51,12 +51,12 @@ def load_weight(nc, consts, words, scales, label):
             out=raw_scales[32 * quadrant : 32 * quadrant + 4, :].bitcast(I32),
             in_=scales[0, 4 * quadrant : 4 * quadrant + 4, :].bitcast(I32),
         )
-    w_words = consts.tile([P, 2 * CHANNELS], U8, name="w_words_" + label, align_bytes=64)
+    w_words = consts.tile([P, 2 * CHANNELS], U8, name="w_words_" + label, align_bytes=256)
     nc.vector.tensor_copy(
         out=w_words[:].bitcast(I32).rearrange("p (j h c) -> p j h c", j=QUARTERS, c=2),
         in_=raw_words[:].bitcast(I32).rearrange("p (h j c) -> p j h c", j=QUARTERS, c=2),
     )
-    w_scales = consts.tile([P, CHANNELS], U8, name="w_scales_" + label, align_bytes=64)
+    w_scales = consts.tile([P, CHANNELS], U8, name="w_scales_" + label, align_bytes=256)
     nc.vector.tensor_copy(
         out=w_scales[:].bitcast(I32).rearrange("p (j h) -> p j h", j=QUARTERS),
         in_=raw_scales[:].bitcast(I32).rearrange("p (h j) -> p j h", j=QUARTERS),
@@ -145,7 +145,7 @@ def tile_costvolumeattention17_pa_kernel(
                     nc.tensor.transpose(
                         turned[:, b, u, :], raw[:, b, :].bitcast(F32)[:, u : CHANNELS // 2 : 2], ident[:]
                     )
-            grouped = grouped_pool.tile([P, blocks * P * 4], BF16, name="grouped", align_bytes=64)
+            grouped = grouped_pool.tile([P, blocks * P * 4], BF16, name="grouped", align_bytes=256)
             nc.scalar.copy(
                 out=grouped[:].bitcast(F32).rearrange("p (c b u) -> p c b u", b=blocks, u=2),
                 in_=turned[:].rearrange("p b u c -> p c b u"),
@@ -155,8 +155,8 @@ def tile_costvolumeattention17_pa_kernel(
         def quantise(g):
             grouped = grouped_of[g]
             width = grouped.shape[1] // 4
-            codes = quant.tile([P, width], U32, name="codes_%d" % g, align_bytes=64)
-            scales = quant.tile([P, width], U8, name="scales_%d" % g, align_bytes=64)
+            codes = quant.tile([P, width], U32, name="codes_%d" % g, align_bytes=256)
+            scales = quant.tile([P, width], U8, name="scales_%d" % g, align_bytes=256)
             nc.vector.quantize_mx(out=codes[:].bitcast(FP8X4), scales=scales[:], in_=grouped[:])
             quantised[g] = (codes, scales)
 

@@ -56,9 +56,9 @@ def load_weight(nc, consts, words, scales, label):
         out=w_words[:].bitcast(I32).rearrange("p (j h c) -> p j h c", j=QUARTERS, c=2),
         in_=raw_words[:].bitcast(I32).rearrange("p (h j c) -> p j h c", j=QUARTERS, c=2),
     )
-    w_scales = consts.tile([P, CHANNELS], U8, name="w_scales_" + label, align_bytes=256)
+    w_scales = consts.tile([P, 2 * CHANNELS], U8, name="w_scales_" + label, align_bytes=256)
     nc.vector.tensor_copy(
-        out=w_scales[:].bitcast(I32).rearrange("p (j h) -> p j h", j=QUARTERS),
+        out=w_scales[:].bitcast(I32).rearrange("p (j s) -> p j s", j=QUARTERS)[:, :, 0:HEADS],
         in_=raw_scales[:].bitcast(I32).rearrange("p (h j) -> p j h", j=QUARTERS),
     )
     return w_words, w_scales
@@ -169,7 +169,7 @@ def tile_costvolumeattention17_pa_kernel(
                 nc.tensor.matmul_mx(
                     out=acc[:, i, :],
                     lhsT=w_words[:, 2 * P * j : 2 * P * (j + 1)].bitcast(FP4X4),
-                    lhsT_scale=w_scales[:, P * j : P * (j + 1)],
+                    lhsT_scale=w_scales[:, 2 * P * j : 2 * P * j + P],
                     rhs=codes[:].bitcast(FP8X4),
                     rhs_scale=scales[:],
                     start=True,

from contextlib import ExitStack

import concourse.mybir as mybir
from concourse.masks import make_identity

F32 = mybir.dt.float32
BF16 = mybir.dt.bfloat16
I32 = mybir.dt.int32
U32 = mybir.dt.uint32
U8 = mybir.dt.uint8
FP8X4 = mybir.dt.float8_e4m3fn_x4
FP4X4 = mybir.dt.float4_e2m1fn_x4
ACT = mybir.ActivationFunctionType
ALU = mybir.AluOpType
AXIS = mybir.AxisListType

P = 128
FRAMES = 8
POSITIONS = 784
CHANNELS = 512
HEADS = 32
HEAD_DIM = 16
QUARTERS = 4
RUN = 4
TOKENS = 128
BODY = 768
TAIL = POSITIONS - BODY
LATE_FRAMES = 2
EARLY_PIECE = 512
MAX_INVERSE_NORM = 1.0e12

FLOPS = 2 * FRAMES * POSITIONS * CHANNELS * 2 * HEADS * HEAD_DIM

CHUNKS = BODY // (2 * P)
TURN_LEAD = 3
QUANTISE_LEAD = 3
ADD_LAG = 1
NORM_LAG = 3
SCALE_LAG = 3
GROUPED_BUFS = 3
SQUARES_BUFS = 2
WORK_BUFS = 4

def load_weight(nc, consts, words, scales, label):
    raw_words = consts.tile([P, 2 * CHANNELS], U8, name="raw_words_" + label)
    nc.sync.dma_start(out=raw_words[:].bitcast(I32), in_=words[0].bitcast(I32))
    raw_scales = consts.tile([P, CHANNELS], U8, name="raw_scales_" + label)
    nc.vector.memset(raw_scales[:].bitcast(I32), 0)
    for quadrant in range(4):
        nc.sync.dma_start(
            out=raw_scales[32 * quadrant : 32 * quadrant + 4, :].bitcast(I32),
            in_=scales[0, 4 * quadrant : 4 * quadrant + 4, :].bitcast(I32),
        )
    w_words = consts.tile([P, 2 * CHANNELS], U8, name="w_words_" + label, align_bytes=256)
    nc.vector.tensor_copy(
        out=w_words[:].bitcast(I32).rearrange("p (j h c) -> p j h c", j=QUARTERS, c=2),
        in_=raw_words[:].bitcast(I32).rearrange("p (h j c) -> p j h c", j=QUARTERS, c=2),
    )
    w_scales = consts.tile([P, 2 * CHANNELS], U8, name="w_scales_" + label, align_bytes=256)
    nc.vector.tensor_copy(
        out=w_scales[:].bitcast(I32).rearrange("p (j s) -> p j s", j=QUARTERS)[:, :, 0:HEADS],
        in_=raw_scales[:].bitcast(I32).rearrange("p (h j) -> p j h", j=QUARTERS),
    )
    return w_words, w_scales


def tile_costvolumeattention17_pa_kernel(
    tc, x, q_w_words, q_w_scales, k_w_words, k_w_scales, out_0, out_1
):
    nc = tc.nc
    tokens = x[0]
    with ExitStack() as ctx:
        consts = ctx.enter_context(tc.tile_pool(name="consts", bufs=1))
        x_pool = ctx.enter_context(tc.tile_pool(name="x_pool", bufs=1))
        quant = ctx.enter_context(tc.tile_pool(name="quant", bufs=1))
        grouped_pool = ctx.enter_context(tc.tile_pool(name="grouped_pool", bufs=GROUPED_BUFS))
        squares_pool = ctx.enter_context(tc.tile_pool(name="squares_pool", bufs=SQUARES_BUFS))
        work = ctx.enter_context(tc.tile_pool(name="work", bufs=WORK_BUFS))
        pairs_pool = ctx.enter_context(tc.tile_pool(name="pairs_pool", bufs=1))
        frames_out = ctx.enter_context(tc.tile_pool(name="frames_out", bufs=4))
        psum = ctx.enter_context(tc.psum_pool(name="psum", bufs=8))
        ctx.enter_context(tc.manual_schedule())

        groups = [("tail", ("q", "k"), None, 0)]
        for f in reversed(range(FRAMES)):
            for s in range(CHUNKS):
                groups.append(((f, s), ("q", "k") if f > 0 else ("q",), f, s * 2 * P))

        x_raw = {}
        x_raw["tail"] = x_pool.tile([P, 1, CHANNELS], BF16, name="x_tail")
        nc.sync.dma_start(
            out=x_raw["tail"][:, 0, :],
            in_=tokens.rearrange("(t n) c -> t n c", t=FRAMES)[:, BODY:POSITIONS, :],
        )
        weights = {
            "q": load_weight(nc, consts, q_w_words, q_w_scales, "q"),
            "k": load_weight(nc, consts, k_w_words, k_w_scales, "k"),
        }
        for chunk, names, f, first in groups[1:]:
            x_raw[chunk] = x_pool.tile([P, 2, CHANNELS], BF16, name="x_raw_%d_%d" % chunk)
            nc.sync.dma_start(
                out=x_raw[chunk][:],
                in_=tokens[f * POSITIONS + first : f * POSITIONS + first + 2 * P, :].rearrange(
                    "(p b) c -> p b c", b=2
                ),
            )

        ident = consts.tile([P, P], F32, name="ident")
        make_identity(nc, ident[:])
        group_sel = consts.tile([P, HEADS], F32, name="group_sel")
        nc.vector.tensor_reduce(
            out=group_sel[:], in_=ident[:].rearrange("p (g r) -> p g r", r=RUN), axis=AXIS.X, op=ALU.add
        )
        group_ones = consts.tile([P, HEADS, RUN], F32, name="group_ones")
        nc.vector.tensor_copy(out=group_ones[:], in_=group_sel[:].unsqueeze(2).to_broadcast([P, HEADS, RUN]))
        tails = {
            "q": consts.tile([P, QUARTERS, FRAMES, TAIL], F32, name="tails_q"),
            "k": consts.tile([P, QUARTERS, FRAMES, TAIL], F32, name="tails_k"),
        }
        rows = {
            "q": out_0.rearrange("(h t) (j r) a b -> t j h r (a b)", t=FRAMES, r=RUN),
            "k": out_1.rearrange("(h t) (j r) a b -> t j h r (a b)", t=FRAMES, r=RUN),
        }

        grouped_of = {}
        quantised = {}
        squares_of = {}
        pairs_of = {}
        partial_of = {}
        inverse_of = {}
        result = {}

        def valid(g):
            return 0 <= g < len(groups)

        def banks(g):
            return 2 * len(groups[g][1]) if valid(g) else 0

        def turn(g):
            raw = x_raw[groups[g][0]]
            blocks = raw.shape[1]
            turned = psum.tile([P, blocks, 2, P], F32, name="turned", tag="bank")
            for b in range(blocks):
                for u in range(2):
                    nc.tensor.transpose(
                        turned[:, b, u, :], raw[:, b, :].bitcast(F32)[:, u : CHANNELS // 2 : 2], ident[:]
                    )
            grouped = grouped_pool.tile([P, blocks * P * 4], BF16, name="grouped", align_bytes=256)
            nc.scalar.copy(
                out=grouped[:].bitcast(F32).rearrange("p (c b u) -> p c b u", b=blocks, u=2),
                in_=turned[:].rearrange("p b u c -> p c b u"),
            )
            grouped_of[g] = grouped

        def quantise(g):
            grouped = grouped_of[g]
            width = grouped.shape[1] // 4
            codes = quant.tile([P, width], U32, name="codes_%d" % g, align_bytes=256)
            scales = quant.tile([P, width], U8, name="scales_%d" % g, align_bytes=256)
            nc.vector.quantize_mx(out=codes[:].bitcast(FP8X4), scales=scales[:], in_=grouped[:])
            quantised[g] = (codes, scales)

        def project(g, bank):
            codes, scales = quantised[g]
            w_words, w_scales = weights[groups[g][1][bank // 2]]
            acc = psum.tile([P, 2, codes.shape[1]], F32, name="acc", tag="bank")
            for i in range(2):
                j = 2 * (bank % 2) + i
                nc.tensor.matmul_mx(
                    out=acc[:, i, :],
                    lhsT=w_words[:, 2 * P * j : 2 * P * (j + 1)].bitcast(FP4X4),
                    lhsT_scale=w_scales[:, 2 * P * j : 2 * P * j + P],
                    rhs=codes[:].bitcast(FP8X4),
                    rhs_scale=scales[:],
                    start=True,
                    stop=True,
                )
            return acc

        def square_bank(g, bank):
            if bank == 0:
                width = quantised[g][0].shape[1]
                squares_of[g] = squares_pool.tile([P, banks(g), 2, width], F32, name="squares")
            acc = project(g, bank)
            nc.scalar.activation(out=squares_of[g][:, bank, :, :], in_=acc[:], func=ACT.Square)

        def add_quarters(g):
            by_weight = squares_of[g][:].rearrange("p (w b) i n -> p w b (i n)", b=2)
            pairs = pairs_pool.tile([P, by_weight.shape[1], by_weight.shape[3]], F32, name="pairs", tag="pairs")
            nc.gpsimd.tensor_tensor(out=pairs[:], in0=by_weight[:, :, 0, :], in1=by_weight[:, :, 1, :], op=ALU.add)
            pairs_of[g] = pairs

        def add_pairs(g):
            halves = pairs_of[g][:].rearrange("p w (i n) -> p w i n", i=2)
            partial = work.tile([P, halves.shape[1], halves.shape[3]], F32, name="partial", tag="partial")
            nc.vector.tensor_tensor(out=partial[:], in0=halves[:, :, 0, :], in1=halves[:, :, 1, :], op=ALU.add)
            partial_of[g] = partial

        def invert_norm(g):
            partial = partial_of[g]
            total = psum.tile(list(partial.shape), F32, name="total", tag="bank")
            nc.tensor.matmul(
                out=total[:].rearrange("p w n -> p (w n)"),
                lhsT=group_ones[:].rearrange("p g r -> p (g r)"),
                rhs=partial[:].rearrange("p w n -> p (w n)"),
                start=True,
                stop=True,
            )
            inverse = work.tile(list(partial.shape), F32, name="inverse", tag="inverse")
            nc.scalar.activation(out=inverse[:], in_=total[:], func=ACT.Abs_reciprocal_sqrt)
            inverse_of[g] = inverse

        def scale_bank(g, bank):
            chunk, names, frame, first = groups[g]
            name = names[bank // 2]
            inverse = inverse_of[g]
            width = inverse.shape[2]
            if frame is None:
                dest = tails[name][:].rearrange("p j t i -> p j (t i)")
            else:
                if first == 0 and bank % 2 == 0:
                    result[name] = frames_out.tile([P, QUARTERS, POSITIONS], F32, name="result")
                    nc.gpsimd.tensor_copy(out=result[name][:, :, BODY:POSITIONS], in_=tails[name][:, :, frame, :])
                dest = result[name][:, :, first : first + width]
            acc = project(g, bank)
            nc.vector.scalar_tensor_tensor(
                out=dest[:, 2 * (bank % 2) : 2 * (bank % 2) + 2, :],
                in0=inverse[:, bank // 2, :].unsqueeze(1).to_broadcast([P, 2, width]),
                scalar=MAX_INVERSE_NORM,
                in1=acc[:],
                op0=ALU.min,
                op1=ALU.mult,
            )
            early = frame is not None and frame < LATE_FRAMES
            if early and first + width == EARLY_PIECE:
                piece = (0, EARLY_PIECE)
            elif frame is not None and first + width == BODY:
                piece = (EARLY_PIECE if early else 0, POSITIONS)
            else:
                piece = None
            if piece is not None:
                if name == "q":
                    targets = [frame]
                elif frame == FRAMES - 1:
                    targets = [frame - 1, frame]
                else:
                    targets = [frame - 1]
                for t in targets:
                    for j in range(2 * (bank % 2), 2 * (bank % 2) + 2):
                        nc.sync.dma_start(
                            out=rows[name][t, j][:, :, piece[0] : piece[1]],
                            in_=result[name][:, j, piece[0] : piece[1]],
                        )

        for step in range(-TURN_LEAD, len(groups) + SCALE_LAG):
            if valid(step + TURN_LEAD):
                turn(step + TURN_LEAD)
            if valid(step - NORM_LAG):
                invert_norm(step - NORM_LAG)
            for bank in range(max(banks(step), banks(step - SCALE_LAG))):
                if bank < banks(step):
                    square_bank(step, bank)
                if bank < banks(step - SCALE_LAG):
                    scale_bank(step - SCALE_LAG, bank)
            if valid(step - ADD_LAG):
                add_pairs(step - ADD_LAG)
            if valid(step + QUANTISE_LEAD):
                quantise(step + QUANTISE_LEAD)
            if valid(step):
                add_quarters(step)
